import numpy as np
import ml_dtypes


def mxq(x, axis, fmt="e4m3"):
    dtype, down = {"e4m3": (ml_dtypes.float8_e4m3fn, 7), "e5m2": (ml_dtypes.float8_e5m2, 14)}[fmt]
    v = np.moveaxis(np.asarray(x, np.float32).astype(ml_dtypes.bfloat16).astype(np.float64), axis, -1)
    blocks = v.reshape(v.shape[:-1] + (-1, 32))
    amax = np.abs(blocks).max(-1, keepdims=True)
    byte = np.maximum(np.where(amax > 0, np.frexp(amax)[1] - 1 + 127, 0) - down, 1)
    scale = np.exp2(byte - 127.0)
    codes = (blocks / scale).astype(np.float32).astype(dtype).astype(np.float64)
    return np.moveaxis((codes * scale).reshape(v.shape), -1, axis)


WIDE = False


def mx_kscale(k):
    if not WIDE:
        return np.ones(k)
    levels = np.array([10, -10, 5, -5, 0])
    a = np.random.permutation(np.resize(levels, k // 512 * 4)).reshape(k // 512, 4)
    idx = np.arange(k)
    return np.exp2(a[idx // 512, idx % 128 // 32])


BF16 = ml_dtypes.bfloat16


def bf(x):
    return np.asarray(x, np.float32).astype(BF16)


def f64(x):
    return np.asarray(x).astype(np.float64)


BS, BLOCK, HID, GAP, G = 256, 512, 1024, 64, 8


def elu(v):
    return np.where(v > 0.0, v, np.exp(np.minimum(v, 0.0)) - 1.0)


def setup_inputs():
    s = mx_kscale(BLOCK)
    s = s / s.max()
    return {"y_lanes": bf((np.random.standard_normal((BS, BLOCK, G)) * 1.3 * s[None, :, None]).reshape(BS, BLOCK * G)),
            "w1": bf(np.random.standard_normal((G, BLOCK, HID)) / np.sqrt(BLOCK) / s[None, :, None]),
            "b1": bf(np.random.standard_normal((G, 1, HID)) * 0.2),
            "w2": bf(np.random.standard_normal((G, HID, BLOCK)) / np.sqrt(HID)),
            "b2": bf(np.random.standard_normal((G, 1, BLOCK)) * 0.2)}


def reference(y_lanes, w1, b1, w2, b2):
    y = f64(y_lanes)
    bs = y.shape[0]
    y = y.reshape(-1, BLOCK, G).transpose(0, 2, 1).reshape(bs, -1)
    z = y.reshape(bs, -1, BLOCK).transpose(1, 0, 2)
    h = elu((mxq(z, 2, "e4m3") @ mxq(f64(w1), 1, "e4m3")) + f64(b1))
    h = (mxq(h, 2, "e4m3") @ mxq(f64(w2), 1, "e4m3")) + f64(b2)
    z = h + z
    y = z.transpose(1, 0, 2).reshape(bs, -1)
    return y.reshape(-1, G, BLOCK).transpose(0, 2, 1).reshape(bs, -1)

@@ -1,0 +1,302 @@
+from contextlib import ExitStack
+
+import concourse.mybir as mybir
+from concourse.masks import make_identity
+
+F32 = mybir.dt.float32
+BF16 = mybir.dt.bfloat16
+U32 = mybir.dt.uint32
+U8 = mybir.dt.uint8
+FP8X4 = mybir.dt.float8_e4m3fn_x4
+ACT = mybir.ActivationFunctionType
+ALU = mybir.AluOpType
+
+P = 128
+BS, BLOCK, HID, G = 256, 512, 1024, 8
+FLOPS = 2 * G * BS * BLOCK * HID * 2
+
+PINNED = True
+S_COLS_A = [336, 336, 96, 96, 96, 96, 96, 96]
+S_ROWS_B = [2, 2, 4, 4, 4, 4, 4, 4]
+
+
+def tile_blockresmlp_mixerblock_pa_kernel(tc, y_lanes, w1, b1, w2, b2, out):
+    nc = tc.nc
+    with ExitStack() as ctx:
+        const = ctx.enter_context(tc.tile_pool(name="const", bufs=1))
+        raw_pool = ctx.enter_context(tc.tile_pool(name="raw", bufs=3))
+        grp_pool = ctx.enter_context(tc.tile_pool(name="grp", bufs=3))
+        code_pool = ctx.enter_context(tc.tile_pool(name="code", bufs=2))
+        act_pool = ctx.enter_context(tc.tile_pool(name="act", bufs=3))
+        work = ctx.enter_context(tc.tile_pool(name="work", bufs=2))
+        psum = ctx.enter_context(tc.psum_pool(name="psum", bufs=2))
+        if PINNED:
+            ctx.enter_context(tc.manual_schedule())
+
+        ident_b = const.tile([P, P], BF16, name="ident_b")
+        ident_f = const.tile([P, P], F32, name="ident_f")
+        make_identity(nc, ident_b[:])
+        make_identity(nc, ident_f[:])
+
+        y_sb = [const.tile([P, BLOCK * G], BF16, name="y_sb%d" % bt) for bt in range(2)]
+        w2raw = const.tile([P, 2 * G, 4, BLOCK], BF16, name="w2raw")
+        zc = const.tile([P, G, BS], U32, name="zc", align_bytes=64)
+        zs = const.tile([P, G, BS], U8, name="zs", align_bytes=64)
+        hc = const.tile([P, G, 2 * BS], U32, name="hc", align_bytes=64)
+        hs = const.tile([P, G, 2 * BS], U8, name="hs", align_bytes=64)
+        brow = const.tile([P, P], BF16, name="brow")
+        bT = const.tile([P, 96], F32, name="bT")
+
+        w1raw = {}
+        grp = {}
+        wc = {}
+        ws = {}
+        zt = {}
+        zg = {}
+        hp = {}
+        e_t = {}
+        r_t = {}
+        hg = {}
+        rp = {}
+        t_t = {}
+        ot = {}
+        osb = {}
+
+        def load_w1(g):
+            w1raw[g] = raw_pool.tile([P, 4, HID], BF16, name="w1raw%d" % g, tag="w1raw")
+            nc.sync.dma_start(out=w1raw[g][:], in_=w1[g].rearrange("(p j) n -> p j n", j=4))
+
+        def load_w2(g):
+            nc.sync.dma_start(
+                out=w2raw[:, 2 * g : 2 * g + 2, :, :],
+                in_=w2[g].rearrange("(c j p) d -> p c j d", c=2, j=4),
+            )
+
+        def regroup(i):
+            grp[i] = grp_pool.tile([P, 1024, 4], BF16, name="grp%d" % i, tag="grp", align_bytes=64)
+            if i < G:
+                nv = HID - S_COLS_A[i]
+                nc.vector.tensor_copy(
+                    out=grp[i][:, 0:nv, :].rearrange("p (c i) t -> p c t i", i=4),
+                    in_=w1raw[i][:, :, 0:nv].rearrange("p t (c i) -> p c t i", i=4),
+                )
+                nc.scalar.copy(
+                    out=grp[i][:, nv:HID, :].rearrange("p (c i) t -> p c t i", i=4),
+                    in_=w1raw[i][:, :, nv:HID].rearrange("p t (c i) -> p c t i", i=4),
+                )
+            else:
+                u = i - G
+                dt, q = u // 2, u % 2
+                rv = 8 - S_ROWS_B[u]
+                dsl = slice(dt * P, (dt + 1) * P)
+                nc.vector.tensor_copy(
+                    out=grp[i][:, 0 : rv * P, :].rearrange("p (r c i) t -> p r c t i", r=rv, i=4),
+                    in_=w2raw[:, 8 * q : 8 * q + rv, :, dsl].rearrange("p r t (c i) -> p r c t i", i=4),
+                )
+                for r in range(rv, 8):
+                    nc.scalar.copy(
+                        out=grp[i][:, r * P : (r + 1) * P, :].rearrange("p (c i) t -> p c t i", i=4),
+                        in_=w2raw[:, 8 * q + r, :, dsl].rearrange("p t (c i) -> p c t i", i=4),
+                    )
+
+        def quant_w(i):
+            wc[i] = code_pool.tile([P, 1024], U32, name="wc%d" % i, tag="wc", align_bytes=64)
+            ws[i] = code_pool.tile([P, 1024], U8, name="ws%d" % i, tag="ws", align_bytes=64)
+            nc.vector.quantize_mx(
+                out=wc[i][:].bitcast(FP8X4),
+                scales=ws[i][:],
+                in_=grp[i][:].rearrange("p n j -> p (n j)"),
+            )
+
+        def z_transposes(g):
+            zt[g] = psum.tile([P, 4, BS], BF16, name="zt%d" % g, tag="zt")
+            for bt in range(2):
+                yv = y_sb[bt][:].rearrange("b (p j g) -> b j g p", j=4, g=G)
+                for j in range(4):
+                    nc.tensor.transpose(
+                        out=zt[g][:, j, bt * P : (bt + 1) * P], in_=yv[:, j, g, :], identity=ident_b[:]
+                    )
+
+        def z_evac(g):
+            zg[g] = work.tile([P, BS, 4], BF16, name="zg%d" % g, tag="zg", align_bytes=64)
+            nc.scalar.copy(out=zg[g][:], in_=zt[g][:].rearrange("p j b -> p b j"))
+
+        def quant_z(g):
+            nc.vector.quantize_mx(
+                out=zc[:, g, :].bitcast(FP8X4),
+                scales=zs[:, g, :],
+                in_=zg[g][:].rearrange("p b j -> p (b j)"),
+            )
+
+        def mm1(g, k):
+            hp[(g, k)] = psum.tile([P, 2, BS], F32, name="hp%d_%d" % (g, k), tag="hp")
+            for h in range(2):
+                t = 2 * k + h
+                nc.tensor.matmul_mx(
+                    out=hp[(g, k)][:, h, :],
+                    lhsT=wc[g][:, t * P : (t + 1) * P].bitcast(FP8X4),
+                    lhsT_scale=ws[g][:, t * P : (t + 1) * P],
+                    rhs=zc[:, g, :].bitcast(FP8X4),
+                    rhs_scale=zs[:, g, :],
+                    start=True,
+                    stop=True,
+                )
+
+        def elu_scalar(g, k):
+            c = k // 2
+            if k % 2 == 0:
+                e_t[(g, c)] = act_pool.tile([P, 4, BS], F32, name="e%d_%d" % (g, c), tag="e")
+                r_t[(g, c)] = act_pool.tile([P, 4, BS], BF16, name="r%d_%d" % (g, c), tag="r")
+            for h in range(2):
+                t = 2 * k + h
+                j = t % 4
+                bias = bT[:, 8 * g + t : 8 * g + t + 1]
+                nc.scalar.activation(
+                    out=e_t[(g, c)][:, j, :], in_=hp[(g, k)][:, h, :], func=ACT.Exp, bias=bias, scale=1.0
+                )
+                nc.scalar.activation(
+                    out=r_t[(g, c)][:, j, :], in_=hp[(g, k)][:, h, :], func=ACT.Relu, bias=bias, scale=1.0
+                )
+
+        def elu_combine(g, c):
+            if c == 0:
+                hg[g] = work.tile([P, 2, BS, 4], BF16, name="hg%d" % g, tag="hg", align_bytes=64)
+            nc.vector.scalar_tensor_tensor(
+                out=hg[g][:, c, :, :],
+                in0=e_t[(g, c)][:].rearrange("p j b -> p b j"),
+                scalar=-1.0,
+                in1=r_t[(g, c)][:].rearrange("p j b -> p b j"),
+                op0=ALU.add,
+                op1=ALU.min,
+            )
+
+        def quant_h(g):
+            nc.vector.quantize_mx(
+                out=hc[:, g, :].bitcast(FP8X4),
+                scales=hs[:, g, :],
+                in_=hg[g][:].rearrange("p c b j -> p (c b j)"),
+            )
+
+        def mm2(u):
+            q = u % 2
+            i = u + G
+            for half in range(2):
+                rp[(u, half)] = psum.tile([P, 2, BS], F32, name="rp%d_%d" % (u, half), tag="rp")
+                for h in range(2):
+                    gl = 2 * half + h
+                    g = 4 * q + gl
+                    for c in range(2):
+                        r = 2 * gl + c
+                        nc.tensor.matmul_mx(
+                            out=rp[(u, half)][:, h, :],
+                            lhsT=wc[i][:, r * P : (r + 1) * P].bitcast(FP8X4),
+                            lhsT_scale=ws[i][:, r * P : (r + 1) * P],
+                            rhs=hc[:, g, c * BS : (c + 1) * BS].bitcast(FP8X4),
+                            rhs_scale=hs[:, g, c * BS : (c + 1) * BS],
+                            start=(c == 0),
+                            stop=(c == 1),
+                        )
+
+        def out_evac(u):
+            dt, q = u // 2, u % 2
+            t_t[u] = work.tile([P, 4, BS], F32, name="t%d" % u, tag="t")
+            for gl in range(4):
+                g = 4 * q + gl
+                col = 64 + 4 * g + dt
+                nc.scalar.activation(
+                    out=t_t[u][:, gl, :],
+                    in_=rp[(u, gl // 2)][:, gl % 2, :],
+                    func=ACT.Identity,
+                    bias=bT[:, col : col + 1],
+                    scale=1.0,
+                )
+
+        def out_transposes(u):
+            for bt in range(2):
+                ot[(u, bt)] = psum.tile([P, 4, P], F32, name="ot%d_%d" % (u, bt), tag="ot")
+                for gl in range(4):
+                    nc.tensor.transpose(
+                        out=ot[(u, bt)][:, gl, :],
+                        in_=t_t[u][:, gl, bt * P : (bt + 1) * P],
+                        identity=ident_f[:],
+                    )
+
+        def out_add(u):
+            dt, q = u // 2, u % 2
+            if q == 0:
+                osb[dt] = work.tile([P, 2, P, G], F32, name="osb%d" % dt, tag="osb")
+            for bt in range(2):
+                yv = y_sb[bt][:].rearrange("b (d g) -> b d g", g=G)
+                nc.vector.tensor_tensor(
+                    out=osb[dt][:, bt, :, 4 * q : 4 * q + 4],
+                    in0=ot[(u, bt)][:].rearrange("p g d -> p d g"),
+                    in1=yv[:, dt * P : (dt + 1) * P, 4 * q : 4 * q + 4],
+                    op=ALU.add,
+                )
+            if q == 1:
+                for bt in range(2):
+                    nc.sync.dma_start(
+                        out=out[bt * P : (bt + 1) * P, dt * P * G : (dt + 1) * P * G],
+                        in_=osb[dt][:, bt, :, :].rearrange("p d g -> p (d g)"),
+                    )
+
+        load_w1(0)
+        for bt in range(2):
+            nc.sync.dma_start(out=y_sb[bt][:], in_=y_lanes[bt * P : (bt + 1) * P, :])
+        nc.vector.memset(brow[96:128, :], 0.0)
+        nc.sync.dma_start(out=brow[0:64, :], in_=b1.rearrange("g o (t p) -> (g o t) p", p=P))
+        nc.sync.dma_start(out=brow[64:96, :], in_=b2.rearrange("g o (t p) -> (g o t) p", p=P))
+        load_w1(1)
+        load_w1(2)
+
+        regroup(0)
+        load_w1(3)
+        quant_w(0)
+        bps = psum.tile([P, P], BF16, name="bps", tag="zt")
+        nc.tensor.transpose(out=bps[:], in_=brow[:], identity=ident_b[:])
+        nc.vector.tensor_copy(out=bT[:], in_=bps[:, 0:96])
+        z_transposes(0)
+        z_evac(0)
+        regroup(1)
+        load_w1(4)
+        load_w2(0)
+        load_w2(1)
+        quant_z(0)
+        z_transposes(1)
+        z_evac(1)
+
+        for s in range(16):
+            if 1 <= s <= 8:
+                elu_combine(s - 1, 1)
+            if s + 1 <= 15:
+                quant_w(s + 1)
+            if 1 <= s <= 8:
+                quant_h(s - 1)
+            if s + 1 <= 7:
+                quant_z(s + 1)
+            if s <= 7:
+                mm1(s, 0)
+                mm1(s, 1)
+                elu_scalar(s, 0)
+                elu_scalar(s, 1)
+            else:
+                mm2(s - 8)
+                out_evac(s - 8)
+                out_transposes(s - 8)
+            if s + 2 <= 15:
+                regroup(s + 2)
+                if s + 5 <= 7:
+                    load_w1(s + 5)
+                    load_w2(2 * s + 2)
+                    load_w2(2 * s + 3)
+            if s + 2 <= 7:
+                z_transposes(s + 2)
+                z_evac(s + 2)
+            if s <= 7:
+                mm1(s, 2)
+                mm1(s, 3)
+                elu_scalar(s, 2)
+                elu_scalar(s, 3)
+                elu_combine(s, 0)
+            else:
+                out_add(s - 8)

@@ -15,9 +15,12 @@ P = 128
 BS, BLOCK, HID, G = 256, 512, 1024, 8
 FLOPS = 2 * G * BS * BLOCK * HID * 2
 
-PINNED = True
-S_COLS_A = [336, 336, 96, 96, 96, 96, 96, 96]
-S_ROWS_B = [2, 2, 4, 4, 4, 4, 4, 4]
+N_A = 16
+N_B = 8
+N_STEPS = N_A + N_B
+S_ROWS_EARLY = 1
+S_ROWS = 4
+W2_AFTER_W1 = {3: (0, 1), 4: (2, 3), 5: (4, 5), 7: (6, 7)}
 
 
 def tile_blockresmlp_mixerblock_pa_kernel(tc, y_lanes, w1, b1, w2, b2, out):
@@ -30,13 +33,12 @@ def tile_blockresmlp_mixerblock_pa_kernel(tc, y_lanes, w1, b1, w2, b2, out):
         act_pool = ctx.enter_context(tc.tile_pool(name="act", bufs=3))
         work = ctx.enter_context(tc.tile_pool(name="work", bufs=2))
         psum = ctx.enter_context(tc.psum_pool(name="psum", bufs=2))
-        if PINNED:
-            ctx.enter_context(tc.manual_schedule())
+        ctx.enter_context(tc.manual_schedule())
 
         ident_b = const.tile([P, P], BF16, name="ident_b")
         ident_f = const.tile([P, P], F32, name="ident_f")
-        make_identity(nc, ident_b[:])
         make_identity(nc, ident_f[:])
+        make_identity(nc, ident_b[:])
 
         y_sb = [const.tile([P, BLOCK * G], BF16, name="y_sb%d" % bt) for bt in range(2)]
         w2raw = const.tile([P, 2 * G, 4, BLOCK], BF16, name="w2raw")
@@ -62,9 +64,17 @@ def tile_blockresmlp_mixerblock_pa_kernel(tc, y_lanes, w1, b1, w2, b2, out):
         ot = {}
         osb = {}
 
-        def load_w1(g):
+        def load_w1(g, pieces):
             w1raw[g] = raw_pool.tile([P, 4, HID], BF16, name="w1raw%d" % g, tag="w1raw")
-            nc.sync.dma_start(out=w1raw[g][:], in_=w1[g].rearrange("(p j) n -> p j n", j=4))
+            src = w1[g].rearrange("(p j) n -> p j n", j=4)
+            return [
+                (w1raw[g][:, :, k * HID // pieces : (k + 1) * HID // pieces],
+                 src[:, :, k * HID // pieces : (k + 1) * HID // pieces])
+                for k in range(pieces)
+            ]
+
+        def start_load(pair):
+            nc.sync.dma_start(out=pair[0], in_=pair[1])
 
         def load_w2(g):
             nc.sync.dma_start(
@@ -73,21 +83,18 @@ def tile_blockresmlp_mixerblock_pa_kernel(tc, y_lanes, w1, b1, w2, b2, out):
             )
 
         def regroup(i):
-            grp[i] = grp_pool.tile([P, 1024, 4], BF16, name="grp%d" % i, tag="grp", align_bytes=64)
-            if i < G:
-                nv = HID - S_COLS_A[i]
+            if i < N_A:
+                g, c = i // 2, i % 2
+                grp[i] = grp_pool.tile([P, 512, 4], BF16, name="grp%d" % i, tag="grp", align_bytes=64)
                 nc.vector.tensor_copy(
-                    out=grp[i][:, 0:nv, :].rearrange("p (c i) t -> p c t i", i=4),
-                    in_=w1raw[i][:, :, 0:nv].rearrange("p t (c i) -> p c t i", i=4),
-                )
-                nc.scalar.copy(
-                    out=grp[i][:, nv:HID, :].rearrange("p (c i) t -> p c t i", i=4),
-                    in_=w1raw[i][:, :, nv:HID].rearrange("p t (c i) -> p c t i", i=4),
+                    out=grp[i][:].rearrange("p (c i) t -> p c t i", i=4),
+                    in_=w1raw[g][:, :, c * 512 : (c + 1) * 512].rearrange("p t (c i) -> p c t i", i=4),
                 )
             else:
-                u = i - G
+                u = i - N_A
                 dt, q = u // 2, u % 2
-                rv = 8 - S_ROWS_B[u]
+                grp[i] = grp_pool.tile([P, 1024, 4], BF16, name="grp%d" % i, tag="grp", align_bytes=64)
+                rv = 8 - (S_ROWS_EARLY if u < 2 else S_ROWS)
                 dsl = slice(dt * P, (dt + 1) * P)
                 nc.vector.tensor_copy(
                     out=grp[i][:, 0 : rv * P, :].rearrange("p (r c i) t -> p r c t i", r=rv, i=4),
@@ -100,86 +107,90 @@ def tile_blockresmlp_mixerblock_pa_kernel(tc, y_lanes, w1, b1, w2, b2, out):
                     )
 
         def quant_w(i):
-            wc[i] = code_pool.tile([P, 1024], U32, name="wc%d" % i, tag="wc", align_bytes=64)
-            ws[i] = code_pool.tile([P, 1024], U8, name="ws%d" % i, tag="ws", align_bytes=64)
+            n = 512 if i < N_A else 1024
+            wc[i] = code_pool.tile([P, n], U32, name="wc%d" % i, tag="wc", align_bytes=64)
+            ws[i] = code_pool.tile([P, n], U8, name="ws%d" % i, tag="ws", align_bytes=64)
             nc.vector.quantize_mx(
                 out=wc[i][:].bitcast(FP8X4),
                 scales=ws[i][:],
                 in_=grp[i][:].rearrange("p n j -> p (n j)"),
             )
 
-        def z_transposes(g):
-            zt[g] = psum.tile([P, 4, BS], BF16, name="zt%d" % g, tag="zt")
-            for bt in range(2):
-                yv = y_sb[bt][:].rearrange("b (p j g) -> b j g p", j=4, g=G)
-                for j in range(4):
-                    nc.tensor.transpose(
-                        out=zt[g][:, j, bt * P : (bt + 1) * P], in_=yv[:, j, g, :], identity=ident_b[:]
-                    )
+        def z_transposes(m):
+            gp, bt = m // 2, m % 2
+            zt[m] = psum.tile([P, 4, P], F32, name="zt%d" % m, tag="zt")
+            yw = y_sb[bt][:].bitcast(F32).rearrange("b (p j w) -> b j w p", j=4, w=4)
+            for j in range(4):
+                nc.tensor.transpose(out=zt[m][:, j, :], in_=yw[:, j, gp, :], identity=ident_f[:])
 
-        def z_evac(g):
-            zg[g] = work.tile([P, BS, 4], BF16, name="zg%d" % g, tag="zg", align_bytes=64)
-            nc.scalar.copy(out=zg[g][:], in_=zt[g][:].rearrange("p j b -> p b j"))
+        def z_evac(n):
+            m, e = n // 2, n % 2
+            gp, bt = m // 2, m % 2
+            if n % 4 == 0:
+                zg[gp] = work.tile([P, 2, BS, 4], BF16, name="zg%d" % gp, tag="zg", align_bytes=64)
+            src = zt[m][:].rearrange("p j b -> p (j b)").bitcast(BF16).rearrange(
+                "p (j b e) -> p e b j", j=4, e=2
+            )
+            nc.scalar.copy(out=zg[gp][:, e, bt * P : (bt + 1) * P, :], in_=src[:, e, :, :])
 
-        def quant_z(g):
+        def quant_z(gp):
             nc.vector.quantize_mx(
-                out=zc[:, g, :].bitcast(FP8X4),
-                scales=zs[:, g, :],
-                in_=zg[g][:].rearrange("p b j -> p (b j)"),
+                out=zc[:, 2 * gp : 2 * gp + 2, :].rearrange("p g b -> p (g b)").bitcast(FP8X4),
+                scales=zs[:, 2 * gp : 2 * gp + 2, :].rearrange("p g b -> p (g b)"),
+                in_=zg[gp][:].rearrange("p e b j -> p (e b j)"),
             )
 
-        def mm1(g, k):
-            hp[(g, k)] = psum.tile([P, 2, BS], F32, name="hp%d_%d" % (g, k), tag="hp")
+        def mm1(a, k):
+            g = a // 2
+            hp[(a, k)] = psum.tile([P, 2, BS], F32, name="hp%d_%d" % (a, k), tag="hp")
             for h in range(2):
-                t = 2 * k + h
+                j = 2 * k + h
                 nc.tensor.matmul_mx(
-                    out=hp[(g, k)][:, h, :],
-                    lhsT=wc[g][:, t * P : (t + 1) * P].bitcast(FP8X4),
-                    lhsT_scale=ws[g][:, t * P : (t + 1) * P],
+                    out=hp[(a, k)][:, h, :],
+                    lhsT=wc[a][:, j * P : (j + 1) * P].bitcast(FP8X4),
+                    lhsT_scale=ws[a][:, j * P : (j + 1) * P],
                     rhs=zc[:, g, :].bitcast(FP8X4),
                     rhs_scale=zs[:, g, :],
                     start=True,
                     stop=True,
                 )
 
-        def elu_scalar(g, k):
-            c = k // 2
-            if k % 2 == 0:
-                e_t[(g, c)] = act_pool.tile([P, 4, BS], F32, name="e%d_%d" % (g, c), tag="e")
-                r_t[(g, c)] = act_pool.tile([P, 4, BS], BF16, name="r%d_%d" % (g, c), tag="r")
+        def elu_scalar(a, k):
+            if k == 0:
+                e_t[a] = act_pool.tile([P, 4, BS], F32, name="e%d" % a, tag="e")
+                r_t[a] = act_pool.tile([P, 4, BS], BF16, name="r%d" % a, tag="r")
             for h in range(2):
-                t = 2 * k + h
-                j = t % 4
-                bias = bT[:, 8 * g + t : 8 * g + t + 1]
+                j = 2 * k + h
+                bias = bT[:, 4 * a + j : 4 * a + j + 1]
                 nc.scalar.activation(
-                    out=e_t[(g, c)][:, j, :], in_=hp[(g, k)][:, h, :], func=ACT.Exp, bias=bias, scale=1.0
+                    out=e_t[a][:, j, :], in_=hp[(a, k)][:, h, :], func=ACT.Exp, bias=bias, scale=1.0
                 )
                 nc.scalar.activation(
-                    out=r_t[(g, c)][:, j, :], in_=hp[(g, k)][:, h, :], func=ACT.Relu, bias=bias, scale=1.0
+                    out=r_t[a][:, j, :], in_=hp[(a, k)][:, h, :], func=ACT.Relu, bias=bias, scale=1.0
                 )
 
-        def elu_combine(g, c):
-            if c == 0:
-                hg[g] = work.tile([P, 2, BS, 4], BF16, name="hg%d" % g, tag="hg", align_bytes=64)
+        def elu_combine(a):
+            hg[a] = work.tile([P, BS, 4], BF16, name="hg%d" % a, tag="hg", align_bytes=64)
             nc.vector.scalar_tensor_tensor(
-                out=hg[g][:, c, :, :],
-                in0=e_t[(g, c)][:].rearrange("p j b -> p b j"),
+                out=hg[a][:],
+                in0=e_t[a][:].rearrange("p j b -> p b j"),
                 scalar=-1.0,
-                in1=r_t[(g, c)][:].rearrange("p j b -> p b j"),
+                in1=r_t[a][:].rearrange("p j b -> p b j"),
                 op0=ALU.add,
                 op1=ALU.min,
             )
 
-        def quant_h(g):
+        def quant_h(a):
+            g, c = a // 2, a % 2
             nc.vector.quantize_mx(
-                out=hc[:, g, :].bitcast(FP8X4),
-                scales=hs[:, g, :],
-                in_=hg[g][:].rearrange("p c b j -> p (c b j)"),
+                out=hc[:, g, c * BS : (c + 1) * BS].bitcast(FP8X4),
+                scales=hs[:, g, c * BS : (c + 1) * BS],
+                in_=hg[a][:].rearrange("p b j -> p (b j)"),
             )
 
         def mm2(u):
             q = u % 2
-            i = u + G
+            i = u + N_A
             for half in range(2):
                 rp[(u, half)] = psum.tile([P, 2, BS], F32, name="rp%d_%d" % (u, half), tag="rp")
                 for h in range(2):
@@ -201,8 +212,7 @@ def tile_blockresmlp_mixerblock_pa_kernel(tc, y_lanes, w1, b1, w2, b2, out):
             dt, q = u // 2, u % 2
             t_t[u] = work.tile([P, 4, BS], F32, name="t%d" % u, tag="t")
             for gl in range(4):
-                g = 4 * q + gl
-                col = 64 + 4 * g + dt
+                col = 64 + 4 * (4 * q + gl) + dt
                 nc.scalar.activation(
                     out=t_t[u][:, gl, :],
                     in_=rp[(u, gl // 2)][:, gl % 2, :],
@@ -233,70 +243,68 @@ def tile_blockresmlp_mixerblock_pa_kernel(tc, y_lanes, w1, b1, w2, b2, out):
                     in1=yv[:, dt * P : (dt + 1) * P, 4 * q : 4 * q + 4],
                     op=ALU.add,
                 )
-            if q == 1:
-                for bt in range(2):
+                if q == 1:
                     nc.sync.dma_start(
                         out=out[bt * P : (bt + 1) * P, dt * P * G : (dt + 1) * P * G],
                         in_=osb[dt][:, bt, :, :].rearrange("p d g -> p (d g)"),
                     )
 
-        load_w1(0)
+        first = load_w1(0, 2)
+        start_load(first[0])
         for bt in range(2):
             nc.sync.dma_start(out=y_sb[bt][:], in_=y_lanes[bt * P : (bt + 1) * P, :])
+        start_load(first[1])
         nc.vector.memset(brow[96:128, :], 0.0)
         nc.sync.dma_start(out=brow[0:64, :], in_=b1.rearrange("g o (t p) -> (g o t) p", p=P))
         nc.sync.dma_start(out=brow[64:96, :], in_=b2.rearrange("g o (t p) -> (g o t) p", p=P))
-        load_w1(1)
-        load_w1(2)
+        start_load(load_w1(1, 1)[0])
+        start_load(load_w1(2, 1)[0])
 
         regroup(0)
-        load_w1(3)
         quant_w(0)
+        z_transposes(0)
+        z_evac(0)
+        z_evac(1)
+        z_transposes(1)
+        z_evac(2)
+        z_evac(3)
+        regroup(1)
         bps = psum.tile([P, P], BF16, name="bps", tag="zt")
         nc.tensor.transpose(out=bps[:], in_=brow[:], identity=ident_b[:])
         nc.vector.tensor_copy(out=bT[:], in_=bps[:, 0:96])
-        z_transposes(0)
-        z_evac(0)
-        regroup(1)
-        load_w1(4)
-        load_w2(0)
-        load_w2(1)
         quant_z(0)
-        z_transposes(1)
-        z_evac(1)
+        z_transposes(2)
+        z_evac(4)
 
-        for s in range(16):
-            if 1 <= s <= 8:
-                elu_combine(s - 1, 1)
-            if s + 1 <= 15:
+        for s in range(N_STEPS):
+            u = s - N_A
+            if 1 <= s <= N_A:
+                elu_combine(s - 1)
+            if s + 1 < N_STEPS:
                 quant_w(s + 1)
-            if 1 <= s <= 8:
-                quant_h(s - 1)
-            if s + 1 <= 7:
-                quant_z(s + 1)
-            if s <= 7:
+            if s < N_A:
                 mm1(s, 0)
                 mm1(s, 1)
+                if s % 2 == 0 and s <= 8:
+                    z_transposes((s + 6) // 2)
                 elu_scalar(s, 0)
+                if s <= 10:
+                    z_evac(s + 5)
                 elu_scalar(s, 1)
             else:
-                mm2(s - 8)
-                out_evac(s - 8)
-                out_transposes(s - 8)
-            if s + 2 <= 15:
+                mm2(u)
+                out_evac(u)
+                out_transposes(u)
+            if s + 2 < N_STEPS:
                 regroup(s + 2)
-                if s + 5 <= 7:
-                    load_w1(s + 5)
-                    load_w2(2 * s + 2)
-                    load_w2(2 * s + 3)
-            if s + 2 <= 7:
-                z_transposes(s + 2)
-                z_evac(s + 2)
-            if s <= 7:
-                mm1(s, 2)
-                mm1(s, 3)
-                elu_scalar(s, 2)
-                elu_scalar(s, 3)
-                elu_combine(s, 0)
-            else:
-                out_add(s - 8)
+            if s % 2 == 1 and s <= 9:
+                g = (s + 5) // 2
+                start_load(load_w1(g, 1)[0])
+                for k in W2_AFTER_W1.get(g, ()):
+                    load_w2(k)
+            if 1 <= s <= N_A:
+                quant_h(s - 1)
+            if s in (2, 6, 10):
+                quant_z((s + 2) // 4)
+            if s >= N_A:
+                out_add(u)

@@ -15,12 +15,9 @@ P = 128
 BS, BLOCK, HID, G = 256, 512, 1024, 8
 FLOPS = 2 * G * BS * BLOCK * HID * 2
 
-N_A = 16
-N_B = 8
-N_STEPS = N_A + N_B
-S_ROWS_EARLY = 1
-S_ROWS = 4
-W2_AFTER_W1 = {3: (0, 1), 4: (2, 3), 5: (4, 5), 7: (6, 7)}
+N_STEPS = 16
+S_COLS_A = [336, 192, 192, 192, 192, 192, 192, 448]
+S_ROWS_B = [3, 3, 4, 4, 4, 4, 4, 4]
 
 
 def tile_blockresmlp_mixerblock_pa_kernel(tc, y_lanes, w1, b1, w2, b2, out):
@@ -58,23 +55,19 @@ def tile_blockresmlp_mixerblock_pa_kernel(tc, y_lanes, w1, b1, w2, b2, out):
         hp = {}
         e_t = {}
         r_t = {}
+        hb = {}
         hg = {}
         rp = {}
         t_t = {}
         ot = {}
         osb = {}
 
-        def load_w1(g, pieces):
-            w1raw[g] = raw_pool.tile([P, 4, HID], BF16, name="w1raw%d" % g, tag="w1raw")
-            src = w1[g].rearrange("(p j) n -> p j n", j=4)
-            return [
-                (w1raw[g][:, :, k * HID // pieces : (k + 1) * HID // pieces],
-                 src[:, :, k * HID // pieces : (k + 1) * HID // pieces])
-                for k in range(pieces)
-            ]
+        def unit(u):
+            return 2 * (u // 4) + u % 2, (u // 2) % 2
 
-        def start_load(pair):
-            nc.sync.dma_start(out=pair[0], in_=pair[1])
+        def load_w1(g):
+            w1raw[g] = raw_pool.tile([P, 4, HID], BF16, name="w1raw%d" % g, tag="w1raw")
+            nc.sync.dma_start(out=w1raw[g][:], in_=w1[g].rearrange("(p j) n -> p j n", j=4))
 
         def load_w2(g):
             nc.sync.dma_start(
@@ -83,18 +76,21 @@ def tile_blockresmlp_mixerblock_pa_kernel(tc, y_lanes, w1, b1, w2, b2, out):
             )
 
         def regroup(i):
-            if i < N_A:
-                g, c = i // 2, i % 2
-                grp[i] = grp_pool.tile([P, 512, 4], BF16, name="grp%d" % i, tag="grp", align_bytes=64)
+            grp[i] = grp_pool.tile([P, 1024, 4], BF16, name="grp%d" % i, tag="grp", align_bytes=64)
+            if i < G:
+                nv = HID - S_COLS_A[i]
                 nc.vector.tensor_copy(
-                    out=grp[i][:].rearrange("p (c i) t -> p c t i", i=4),
-                    in_=w1raw[g][:, :, c * 512 : (c + 1) * 512].rearrange("p t (c i) -> p c t i", i=4),
+                    out=grp[i][:, 0:nv, :].rearrange("p (c i) t -> p c t i", i=4),
+                    in_=w1raw[i][:, :, 0:nv].rearrange("p t (c i) -> p c t i", i=4),
+                )
+                nc.scalar.copy(
+                    out=grp[i][:, nv:HID, :].rearrange("p (c i) t -> p c t i", i=4),
+                    in_=w1raw[i][:, :, nv:HID].rearrange("p t (c i) -> p c t i", i=4),
                 )
             else:
-                u = i - N_A
-                dt, q = u // 2, u % 2
-                grp[i] = grp_pool.tile([P, 1024, 4], BF16, name="grp%d" % i, tag="grp", align_bytes=64)
-                rv = 8 - (S_ROWS_EARLY if u < 2 else S_ROWS)
+                u = i - G
+                dt, q = unit(u)
+                rv = 8 - S_ROWS_B[u]
                 dsl = slice(dt * P, (dt + 1) * P)
                 nc.vector.tensor_copy(
                     out=grp[i][:, 0 : rv * P, :].rearrange("p (r c i) t -> p r c t i", r=rv, i=4),
@@ -107,9 +103,8 @@ def tile_blockresmlp_mixerblock_pa_kernel(tc, y_lanes, w1, b1, w2, b2, out):
                     )
 
         def quant_w(i):
-            n = 512 if i < N_A else 1024
-            wc[i] = code_pool.tile([P, n], U32, name="wc%d" % i, tag="wc", align_bytes=64)
-            ws[i] = code_pool.tile([P, n], U8, name="ws%d" % i, tag="ws", align_bytes=64)
+            wc[i] = code_pool.tile([P, 1024], U32, name="wc%d" % i, tag="wc", align_bytes=64)
+            ws[i] = code_pool.tile([P, 1024], U8, name="ws%d" % i, tag="ws", align_bytes=64)
             nc.vector.quantize_mx(
                 out=wc[i][:].bitcast(FP8X4),
                 scales=ws[i][:],
@@ -123,15 +118,14 @@ def tile_blockresmlp_mixerblock_pa_kernel(tc, y_lanes, w1, b1, w2, b2, out):
             for j in range(4):
                 nc.tensor.transpose(out=zt[m][:, j, :], in_=yw[:, j, gp, :], identity=ident_f[:])
 
-        def z_evac(n):
-            m, e = n // 2, n % 2
+        def z_evac(m):
             gp, bt = m // 2, m % 2
-            if n % 4 == 0:
+            if bt == 0:
                 zg[gp] = work.tile([P, 2, BS, 4], BF16, name="zg%d" % gp, tag="zg", align_bytes=64)
             src = zt[m][:].rearrange("p j b -> p (j b)").bitcast(BF16).rearrange(
                 "p (j b e) -> p e b j", j=4, e=2
             )
-            nc.scalar.copy(out=zg[gp][:, e, bt * P : (bt + 1) * P, :], in_=src[:, e, :, :])
+            nc.scalar.copy(out=zg[gp][:, :, bt * P : (bt + 1) * P, :], in_=src)
 
         def quant_z(gp):
             nc.vector.quantize_mx(
@@ -140,57 +134,65 @@ def tile_blockresmlp_mixerblock_pa_kernel(tc, y_lanes, w1, b1, w2, b2, out):
                 in_=zg[gp][:].rearrange("p e b j -> p (e b j)"),
             )
 
-        def mm1(a, k):
-            g = a // 2
-            hp[(a, k)] = psum.tile([P, 2, BS], F32, name="hp%d_%d" % (a, k), tag="hp")
+        def mm1(g, k):
+            hp[(g, k)] = psum.tile([P, 2, BS], F32, name="hp%d_%d" % (g, k), tag="hp")
             for h in range(2):
-                j = 2 * k + h
+                t = 2 * k + h
                 nc.tensor.matmul_mx(
-                    out=hp[(a, k)][:, h, :],
-                    lhsT=wc[a][:, j * P : (j + 1) * P].bitcast(FP8X4),
-                    lhsT_scale=ws[a][:, j * P : (j + 1) * P],
+                    out=hp[(g, k)][:, h, :],
+                    lhsT=wc[g][:, t * P : (t + 1) * P].bitcast(FP8X4),
+                    lhsT_scale=ws[g][:, t * P : (t + 1) * P],
                     rhs=zc[:, g, :].bitcast(FP8X4),
                     rhs_scale=zs[:, g, :],
                     start=True,
                     stop=True,
                 )
 
-        def elu_scalar(a, k):
-            if k == 0:
-                e_t[a] = act_pool.tile([P, 4, BS], F32, name="e%d" % a, tag="e")
-                r_t[a] = act_pool.tile([P, 4, BS], BF16, name="r%d" % a, tag="r")
+        def elu_scalar(g, k):
+            c = k // 2
+            if k % 2 == 0:
+                e_t[(g, c)] = act_pool.tile([P, 4, BS], F32, name="e%d_%d" % (g, c), tag="e")
+                r_t[(g, c)] = act_pool.tile([P, 4, BS], BF16, name="r%d_%d" % (g, c), tag="r")
             for h in range(2):
-                j = 2 * k + h
-                bias = bT[:, 4 * a + j : 4 * a + j + 1]
+                t = 2 * k + h
+                j = t % 4
+                bias = bT[:, 8 * g + t : 8 * g + t + 1]
                 nc.scalar.activation(
-                    out=e_t[a][:, j, :], in_=hp[(a, k)][:, h, :], func=ACT.Exp, bias=bias, scale=1.0
+                    out=e_t[(g, c)][:, j, :], in_=hp[(g, k)][:, h, :], func=ACT.Exp, bias=bias, scale=1.0
                 )
                 nc.scalar.activation(
-                    out=r_t[a][:, j, :], in_=hp[(a, k)][:, h, :], func=ACT.Relu, bias=bias, scale=1.0
+                    out=r_t[(g, c)][:, j, :], in_=hp[(g, k)][:, h, :], func=ACT.Relu, bias=bias, scale=1.0
                 )
 
-        def elu_combine(a):
-            hg[a] = work.tile([P, BS, 4], BF16, name="hg%d" % a, tag="hg", align_bytes=64)
+        def elu_combine(g, c):
+            hb[(g, c)] = work.tile([P, 4, BS], BF16, name="hb%d_%d" % (g, c), tag="hb")
             nc.vector.scalar_tensor_tensor(
-                out=hg[a][:],
-                in0=e_t[a][:].rearrange("p j b -> p b j"),
+                out=hb[(g, c)][:].rearrange("p j b -> p (j b)"),
+                in0=e_t[(g, c)][:].rearrange("p j b -> p (j b)"),
                 scalar=-1.0,
-                in1=r_t[a][:].rearrange("p j b -> p b j"),
+                in1=r_t[(g, c)][:].rearrange("p j b -> p (j b)"),
                 op0=ALU.add,
                 op1=ALU.min,
             )
 
-        def quant_h(a):
-            g, c = a // 2, a % 2
+        def h_regroup(g, c):
+            if c == 0:
+                hg[g] = work.tile([P, 2, BS, 4], BF16, name="hg%d" % g, tag="hg", align_bytes=64)
+            nc.vector.tensor_copy(
+                out=hg[g][:, c, :, :].rearrange("p (c i) t -> p c t i", i=4),
+                in_=hb[(g, c)][:].rearrange("p t (c i) -> p c t i", i=4),
+            )
+
+        def quant_h(g):
             nc.vector.quantize_mx(
-                out=hc[:, g, c * BS : (c + 1) * BS].bitcast(FP8X4),
-                scales=hs[:, g, c * BS : (c + 1) * BS],
-                in_=hg[a][:].rearrange("p b j -> p (b j)"),
+                out=hc[:, g, :].bitcast(FP8X4),
+                scales=hs[:, g, :],
+                in_=hg[g][:].rearrange("p c b j -> p (c b j)"),
             )
 
         def mm2(u):
-            q = u % 2
-            i = u + N_A
+            dt, q = unit(u)
+            i = u + G
             for half in range(2):
                 rp[(u, half)] = psum.tile([P, 2, BS], F32, name="rp%d_%d" % (u, half), tag="rp")
                 for h in range(2):
@@ -209,7 +211,7 @@ def tile_blockresmlp_mixerblock_pa_kernel(tc, y_lanes, w1, b1, w2, b2, out):
                         )
 
         def out_evac(u):
-            dt, q = u // 2, u % 2
+            dt, q = unit(u)
             t_t[u] = work.tile([P, 4, BS], F32, name="t%d" % u, tag="t")
             for gl in range(4):
                 col = 64 + 4 * (4 * q + gl) + dt
@@ -232,7 +234,7 @@ def tile_blockresmlp_mixerblock_pa_kernel(tc, y_lanes, w1, b1, w2, b2, out):
                     )
 
         def out_add(u):
-            dt, q = u // 2, u % 2
+            dt, q = unit(u)
             if q == 0:
                 osb[dt] = work.tile([P, 2, P, G], F32, name="osb%d" % dt, tag="osb")
             for bt in range(2):
@@ -249,47 +251,48 @@ def tile_blockresmlp_mixerblock_pa_kernel(tc, y_lanes, w1, b1, w2, b2, out):
                         in_=osb[dt][:, bt, :, :].rearrange("p d g -> p (d g)"),
                     )
 
-        first = load_w1(0, 2)
-        start_load(first[0])
+        load_w1(0)
         for bt in range(2):
             nc.sync.dma_start(out=y_sb[bt][:], in_=y_lanes[bt * P : (bt + 1) * P, :])
-        start_load(first[1])
         nc.vector.memset(brow[96:128, :], 0.0)
         nc.sync.dma_start(out=brow[0:64, :], in_=b1.rearrange("g o (t p) -> (g o t) p", p=P))
         nc.sync.dma_start(out=brow[64:96, :], in_=b2.rearrange("g o (t p) -> (g o t) p", p=P))
-        start_load(load_w1(1, 1)[0])
-        start_load(load_w1(2, 1)[0])
+        load_w1(1)
+        load_w1(2)
 
         regroup(0)
+        load_w1(3)
         quant_w(0)
         z_transposes(0)
         z_evac(0)
-        z_evac(1)
         z_transposes(1)
-        z_evac(2)
-        z_evac(3)
-        regroup(1)
+        z_evac(1)
         bps = psum.tile([P, P], BF16, name="bps", tag="zt")
         nc.tensor.transpose(out=bps[:], in_=brow[:], identity=ident_b[:])
         nc.vector.tensor_copy(out=bT[:], in_=bps[:, 0:96])
         quant_z(0)
+        regroup(1)
+        load_w1(4)
+        load_w2(0)
+        load_w2(1)
         z_transposes(2)
-        z_evac(4)
+        z_evac(2)
 
         for s in range(N_STEPS):
-            u = s - N_A
-            if 1 <= s <= N_A:
-                elu_combine(s - 1)
+            u = s - G
+            if 2 <= s <= 9:
+                quant_h(s - 2)
             if s + 1 < N_STEPS:
                 quant_w(s + 1)
-            if s < N_A:
+            if 1 <= s <= G:
+                h_regroup(s - 1, 0)
+                elu_combine(s - 1, 1)
+            if s < G:
                 mm1(s, 0)
                 mm1(s, 1)
-                if s % 2 == 0 and s <= 8:
-                    z_transposes((s + 6) // 2)
+                if s <= 4:
+                    z_transposes(s + 3)
                 elu_scalar(s, 0)
-                if s <= 10:
-                    z_evac(s + 5)
                 elu_scalar(s, 1)
             else:
                 mm2(u)
@@ -297,14 +300,21 @@ def tile_blockresmlp_mixerblock_pa_kernel(tc, y_lanes, w1, b1, w2, b2, out):
                 out_transposes(u)
             if s + 2 < N_STEPS:
                 regroup(s + 2)
-            if s % 2 == 1 and s <= 9:
-                g = (s + 5) // 2
-                start_load(load_w1(g, 1)[0])
-                for k in W2_AFTER_W1.get(g, ()):
-                    load_w2(k)
-            if 1 <= s <= N_A:
-                quant_h(s - 1)
-            if s in (2, 6, 10):
-                quant_z((s + 2) // 4)
-            if s >= N_A:
+                if s + 5 < G:
+                    load_w1(s + 5)
+                    load_w2(2 * s + 2)
+                    load_w2(2 * s + 3)
+            if s <= 4:
+                z_evac(s + 3)
+            if 1 <= s <= G:
+                h_regroup(s - 1, 1)
+            if s in (0, 2, 4):
+                quant_z(s // 2 + 1)
+            if s < G:
+                mm1(s, 2)
+                mm1(s, 3)
+                elu_scalar(s, 2)
+                elu_scalar(s, 3)
+                elu_combine(s, 0)
+            else:
                 out_add(u)

@@ -16,7 +16,7 @@ BS, BLOCK, HID, G = 256, 512, 1024, 8
 FLOPS = 2 * G * BS * BLOCK * HID * 2
 
 N_STEPS = 16
-S_COLS_A = [336, 192, 192, 192, 192, 192, 192, 448]
+S_COLS_A = [336, 128, 128, 128, 128, 128, 128, 128]
 S_ROWS_B = [3, 3, 4, 4, 4, 4, 4, 4]
 
 
@@ -55,7 +55,6 @@ def tile_blockresmlp_mixerblock_pa_kernel(tc, y_lanes, w1, b1, w2, b2, out):
         hp = {}
         e_t = {}
         r_t = {}
-        hb = {}
         hg = {}
         rp = {}
         t_t = {}
@@ -165,22 +164,15 @@ def tile_blockresmlp_mixerblock_pa_kernel(tc, y_lanes, w1, b1, w2, b2, out):
                 )
 
         def elu_combine(g, c):
-            hb[(g, c)] = work.tile([P, 4, BS], BF16, name="hb%d_%d" % (g, c), tag="hb")
-            nc.vector.scalar_tensor_tensor(
-                out=hb[(g, c)][:].rearrange("p j b -> p (j b)"),
-                in0=e_t[(g, c)][:].rearrange("p j b -> p (j b)"),
-                scalar=-1.0,
-                in1=r_t[(g, c)][:].rearrange("p j b -> p (j b)"),
-                op0=ALU.add,
-                op1=ALU.min,
-            )
-
-        def h_regroup(g, c):
             if c == 0:
                 hg[g] = work.tile([P, 2, BS, 4], BF16, name="hg%d" % g, tag="hg", align_bytes=64)
-            nc.vector.tensor_copy(
-                out=hg[g][:, c, :, :].rearrange("p (c i) t -> p c t i", i=4),
-                in_=hb[(g, c)][:].rearrange("p t (c i) -> p c t i", i=4),
+            nc.vector.scalar_tensor_tensor(
+                out=hg[g][:, c, :, :],
+                in0=e_t[(g, c)][:].rearrange("p j b -> p b j"),
+                scalar=-1.0,
+                in1=r_t[(g, c)][:].rearrange("p j b -> p b j"),
+                op0=ALU.add,
+                op1=ALU.min,
             )
 
         def quant_h(g):
@@ -270,22 +262,19 @@ def tile_blockresmlp_mixerblock_pa_kernel(tc, y_lanes, w1, b1, w2, b2, out):
         bps = psum.tile([P, P], BF16, name="bps", tag="zt")
         nc.tensor.transpose(out=bps[:], in_=brow[:], identity=ident_b[:])
         nc.vector.tensor_copy(out=bT[:], in_=bps[:, 0:96])
+        z_transposes(2)
+        z_evac(2)
         quant_z(0)
         regroup(1)
         load_w1(4)
         load_w2(0)
         load_w2(1)
-        z_transposes(2)
-        z_evac(2)
 
         for s in range(N_STEPS):
             u = s - G
-            if 2 <= s <= 9:
-                quant_h(s - 2)
             if s + 1 < N_STEPS:
                 quant_w(s + 1)
             if 1 <= s <= G:
-                h_regroup(s - 1, 0)
                 elu_combine(s - 1, 1)
             if s < G:
                 mm1(s, 0)
@@ -307,7 +296,7 @@ def tile_blockresmlp_mixerblock_pa_kernel(tc, y_lanes, w1, b1, w2, b2, out):
             if s <= 4:
                 z_evac(s + 3)
             if 1 <= s <= G:
-                h_regroup(s - 1, 1)
+                quant_h(s - 1)
             if s in (0, 2, 4):
                 quant_z(s // 2 + 1)
             if s < G:

@@ -15,7 +15,7 @@ P = 128
 BS, BLOCK, HID, G = 256, 512, 1024, 8
 FLOPS = 2 * G * BS * BLOCK * HID * 2
 
-N_STEPS = 16
+N_UNITS = 16
 S_COLS_A = [336, 128, 128, 128, 128, 128, 128, 128]
 S_ROWS_B = [3, 3, 4, 4, 4, 4, 4, 4]
 
@@ -134,7 +134,7 @@ def tile_blockresmlp_mixerblock_pa_kernel(tc, y_lanes, w1, b1, w2, b2, out):
             )
 
         def mm1(g, k):
-            hp[(g, k)] = psum.tile([P, 2, BS], F32, name="hp%d_%d" % (g, k), tag="hp")
+            hp[(g, k)] = psum.tile([P, 2, BS], F32, name="hp%d_%d" % (g, k), tag="acc", bufs=4)
             for h in range(2):
                 t = 2 * k + h
                 nc.tensor.matmul_mx(
@@ -186,7 +186,7 @@ def tile_blockresmlp_mixerblock_pa_kernel(tc, y_lanes, w1, b1, w2, b2, out):
             dt, q = unit(u)
             i = u + G
             for half in range(2):
-                rp[(u, half)] = psum.tile([P, 2, BS], F32, name="rp%d_%d" % (u, half), tag="rp")
+                rp[(u, half)] = psum.tile([P, 2, BS], F32, name="rp%d_%d" % (u, half), tag="acc", bufs=4)
                 for h in range(2):
                     gl = 2 * half + h
                     g = 4 * q + gl
@@ -265,29 +265,32 @@ def tile_blockresmlp_mixerblock_pa_kernel(tc, y_lanes, w1, b1, w2, b2, out):
         z_transposes(2)
         z_evac(2)
         quant_z(0)
+        for k in range(4):
+            mm1(0, k)
         regroup(1)
         load_w1(4)
         load_w2(0)
         load_w2(1)
 
-        for s in range(N_STEPS):
+        for s in range(N_UNITS + 1):
             u = s - G
-            if s + 1 < N_STEPS:
+            if s + 1 < N_UNITS:
                 quant_w(s + 1)
             if 1 <= s <= G:
                 elu_combine(s - 1, 1)
             if s < G:
-                mm1(s, 0)
-                mm1(s, 1)
                 if s <= 4:
                     z_transposes(s + 3)
-                elu_scalar(s, 0)
-                elu_scalar(s, 1)
+                for k in range(2):
+                    elu_scalar(s, k)
+                    if s + 1 < G:
+                        mm1(s + 1, k)
             else:
-                mm2(u)
-                out_evac(u)
-                out_transposes(u)
-            if s + 2 < N_STEPS:
+                if u < G:
+                    mm2(u)
+                if u >= 1:
+                    out_transposes(u - 1)
+            if s + 2 < N_UNITS:
                 regroup(s + 2)
                 if s + 5 < G:
                     load_w1(s + 5)
@@ -300,10 +303,13 @@ def tile_blockresmlp_mixerblock_pa_kernel(tc, y_lanes, w1, b1, w2, b2, out):
             if s in (0, 2, 4):
                 quant_z(s // 2 + 1)
             if s < G:
-                mm1(s, 2)
-                mm1(s, 3)
-                elu_scalar(s, 2)
-                elu_scalar(s, 3)
+                for k in range(2, 4):
+                    elu_scalar(s, k)
+                    if s + 1 < G:
+                        mm1(s + 1, k)
                 elu_combine(s, 0)
             else:
-                out_add(u)
+                if u < G:
+                    out_evac(u)
+                if u >= 1:
+                    out_add(u - 1)

@@ -16,8 +16,8 @@ BS, BLOCK, HID, G = 256, 512, 1024, 8
 FLOPS = 2 * G * BS * BLOCK * HID * 2
 
 N_UNITS = 16
-S_COLS_A = [336, 128, 128, 128, 128, 128, 128, 128]
-S_ROWS_B = [3, 3, 4, 4, 4, 4, 4, 4]
+S_COLS_A = [160, 160, 160, 160, 160, 160, 160, 160]
+S_ROWS_B = [2, 2, 4, 4, 4, 4, 4, 4]
 
 
 def tile_blockresmlp_mixerblock_pa_kernel(tc, y_lanes, w1, b1, w2, b2, out):

@@ -16,8 +16,10 @@ BS, BLOCK, HID, G = 256, 512, 1024, 8
 FLOPS = 2 * G * BS * BLOCK * HID * 2
 
 N_UNITS = 16
-S_COLS_A = [160, 160, 160, 160, 160, 160, 160, 160]
+S_COLS_A = [160, 160, 256, 256, 256, 256, 256, 256]
 S_ROWS_B = [2, 2, 4, 4, 4, 4, 4, 4]
+PE_TILES = range(2, 14)
+PE_W = 256
 
 
 def tile_blockresmlp_mixerblock_pa_kernel(tc, y_lanes, w1, b1, w2, b2, out):
@@ -60,6 +62,7 @@ def tile_blockresmlp_mixerblock_pa_kernel(tc, y_lanes, w1, b1, w2, b2, out):
         t_t = {}
         ot = {}
         osb = {}
+        pg = {}
 
         def unit(u):
             return 2 * (u // 4) + u % 2, (u // 2) % 2
@@ -74,6 +77,25 @@ def tile_blockresmlp_mixerblock_pa_kernel(tc, y_lanes, w1, b1, w2, b2, out):
                 in_=w2[g].rearrange("(c j p) d -> p c j d", c=2, j=4),
             )
 
+        def regroup_pe(i):
+            if i not in PE_TILES:
+                return
+            pg[i] = psum.tile([P, PE_W, 4], BF16, name="pg%d" % i, tag="ot" if i < G + 2 else "zt")
+            for h in range(PE_W // P):
+                if i < G:
+                    lo = HID - PE_W + h * P
+                    src = w1raw[i][:, :, lo : lo + P]
+                else:
+                    dt, q = unit(i - G)
+                    src = w2raw[:, 8 * q + 8 - PE_W // P + h, :, dt * P : (dt + 1) * P]
+                nc.tensor.matmul(
+                    out=pg[i][:, h * P : (h + 1) * P, :].rearrange("p (c i) t -> p c t i", i=4),
+                    lhsT=ident_b[:],
+                    rhs=src.rearrange("p t (c i) -> p c t i", i=4),
+                    start=True,
+                    stop=True,
+                )
+
         def regroup(i):
             grp[i] = grp_pool.tile([P, 1024, 4], BF16, name="grp%d" % i, tag="grp", align_bytes=64)
             if i < G:
@@ -82,10 +104,11 @@ def tile_blockresmlp_mixerblock_pa_kernel(tc, y_lanes, w1, b1, w2, b2, out):
                     out=grp[i][:, 0:nv, :].rearrange("p (c i) t -> p c t i", i=4),
                     in_=w1raw[i][:, :, 0:nv].rearrange("p t (c i) -> p c t i", i=4),
                 )
-                nc.scalar.copy(
-                    out=grp[i][:, nv:HID, :].rearrange("p (c i) t -> p c t i", i=4),
-                    in_=w1raw[i][:, :, nv:HID].rearrange("p t (c i) -> p c t i", i=4),
-                )
+                if i not in PE_TILES:
+                    nc.scalar.copy(
+                        out=grp[i][:, nv:HID, :].rearrange("p (c i) t -> p c t i", i=4),
+                        in_=w1raw[i][:, :, nv:HID].rearrange("p t (c i) -> p c t i", i=4),
+                    )
             else:
                 u = i - G
                 dt, q = unit(u)
@@ -95,11 +118,14 @@ def tile_blockresmlp_mixerblock_pa_kernel(tc, y_lanes, w1, b1, w2, b2, out):
                     out=grp[i][:, 0 : rv * P, :].rearrange("p (r c i) t -> p r c t i", r=rv, i=4),
                     in_=w2raw[:, 8 * q : 8 * q + rv, :, dsl].rearrange("p r t (c i) -> p r c t i", i=4),
                 )
-                for r in range(rv, 8):
+                for r in range(rv, 6 if i in PE_TILES else 8):
                     nc.scalar.copy(
                         out=grp[i][:, r * P : (r + 1) * P, :].rearrange("p (c i) t -> p c t i", i=4),
                         in_=w2raw[:, 8 * q + r, :, dsl].rearrange("p t (c i) -> p c t i", i=4),
                     )
+
+            if i in PE_TILES:
+                nc.scalar.copy(out=grp[i][:, HID - PE_W : HID, :], in_=pg[i][:])
 
         def quant_w(i):
             wc[i] = code_pool.tile([P, 1024], U32, name="wc%d" % i, tag="wc", align_bytes=64)
@@ -278,6 +304,8 @@ def tile_blockresmlp_mixerblock_pa_kernel(tc, y_lanes, w1, b1, w2, b2, out):
                 quant_w(s + 1)
             if 1 <= s <= G:
                 elu_combine(s - 1, 1)
+            if s + 2 < N_UNITS:
+                regroup_pe(s + 2)
             if s < G:
                 if s <= 4:
                     z_transposes(s + 3)

@@ -16,10 +16,13 @@ BS, BLOCK, HID, G = 256, 512, 1024, 8
 FLOPS = 2 * G * BS * BLOCK * HID * 2
 
 N_UNITS = 16
-S_COLS_A = [160, 160, 256, 256, 256, 256, 256, 256]
-S_ROWS_B = [2, 2, 4, 4, 4, 4, 4, 4]
+S_COLS_A = [0,0,0,64,64,64,64,64]
+S_ROWS_B = [2,2,2,2,4,2,4,4]
 PE_TILES = range(2, 14)
 PE_W = 256
+AHEAD = 2
+PARTS = {0: 2, 2: 2}
+UNITS = [(0, 0), (1, 0), (0, 1), (1, 1), (2, 0), (2, 1), (3, 0), (3, 1)]
 
 
 def tile_blockresmlp_mixerblock_pa_kernel(tc, y_lanes, w1, b1, w2, b2, out):
@@ -28,10 +31,11 @@ def tile_blockresmlp_mixerblock_pa_kernel(tc, y_lanes, w1, b1, w2, b2, out):
         const = ctx.enter_context(tc.tile_pool(name="const", bufs=1))
         raw_pool = ctx.enter_context(tc.tile_pool(name="raw", bufs=3))
         grp_pool = ctx.enter_context(tc.tile_pool(name="grp", bufs=3))
-        code_pool = ctx.enter_context(tc.tile_pool(name="code", bufs=2))
+        code_pool = ctx.enter_context(tc.tile_pool(name="code", bufs=3))
         act_pool = ctx.enter_context(tc.tile_pool(name="act", bufs=3))
+        zh_pool = ctx.enter_context(tc.tile_pool(name="zh", bufs=4))
         work = ctx.enter_context(tc.tile_pool(name="work", bufs=2))
-        psum = ctx.enter_context(tc.psum_pool(name="psum", bufs=2))
+        psum = ctx.enter_context(tc.psum_pool(name="psum", bufs=4))
         ctx.enter_context(tc.manual_schedule())
 
         ident_b = const.tile([P, P], BF16, name="ident_b")
@@ -47,11 +51,13 @@ def tile_blockresmlp_mixerblock_pa_kernel(tc, y_lanes, w1, b1, w2, b2, out):
         hs = const.tile([P, G, 2 * BS], U8, name="hs", align_bytes=64)
         brow = const.tile([P, P], BF16, name="brow")
         bT = const.tile([P, 96], F32, name="bT")
+        warm = const.tile([P, 1], F32, name="warm")
 
         w1raw = {}
         grp = {}
         wc = {}
         ws = {}
+        pg = {}
         zt = {}
         zg = {}
         hp = {}
@@ -62,14 +68,19 @@ def tile_blockresmlp_mixerblock_pa_kernel(tc, y_lanes, w1, b1, w2, b2, out):
         t_t = {}
         ot = {}
         osb = {}
-        pg = {}
 
         def unit(u):
-            return 2 * (u // 4) + u % 2, (u // 2) % 2
+            return UNITS[u]
 
         def load_w1(g):
-            w1raw[g] = raw_pool.tile([P, 4, HID], BF16, name="w1raw%d" % g, tag="w1raw")
-            nc.sync.dma_start(out=w1raw[g][:], in_=w1[g].rearrange("(p j) n -> p j n", j=4))
+            parts = PARTS.get(g, 1)
+            w = HID // parts
+            w1raw[g] = raw_pool.tile([P, parts, 4, w], BF16, name="w1raw%d" % g, tag="w1raw")
+            for h in range(parts):
+                nc.sync.dma_start(
+                    out=w1raw[g][:, h, :, :],
+                    in_=w1[g].rearrange("(p j) n -> p j n", j=4)[:, :, h * w : (h + 1) * w],
+                )
 
         def load_w2(g):
             nc.sync.dma_start(
@@ -80,11 +91,12 @@ def tile_blockresmlp_mixerblock_pa_kernel(tc, y_lanes, w1, b1, w2, b2, out):
         def regroup_pe(i):
             if i not in PE_TILES:
                 return
-            pg[i] = psum.tile([P, PE_W, 4], BF16, name="pg%d" % i, tag="ot" if i < G + 2 else "zt")
+            pg[i] = psum.tile([P, PE_W, 4], BF16, name="pg%d" % i, tag="tr")
             for h in range(PE_W // P):
                 if i < G:
-                    lo = HID - PE_W + h * P
-                    src = w1raw[i][:, :, lo : lo + P]
+                    w = HID // PARTS.get(i, 1)
+                    lo = w - PE_W + h * P
+                    src = w1raw[i][:, PARTS.get(i, 1) - 1, :, lo : lo + P]
                 else:
                     dt, q = unit(i - G)
                     src = w2raw[:, 8 * q + 8 - PE_W // P + h, :, dt * P : (dt + 1) * P]
@@ -96,34 +108,39 @@ def tile_blockresmlp_mixerblock_pa_kernel(tc, y_lanes, w1, b1, w2, b2, out):
                     stop=True,
                 )
 
-        def regroup(i):
-            grp[i] = grp_pool.tile([P, 1024, 4], BF16, name="grp%d" % i, tag="grp", align_bytes=64)
+        def regroup(i, only=None):
+            if i not in grp:
+                grp[i] = grp_pool.tile([P, 1024, 4], BF16, name="grp%d" % i, tag="grp", align_bytes=64)
+            tail = PE_W if i in PE_TILES else 0
             if i < G:
-                nv = HID - S_COLS_A[i]
-                nc.vector.tensor_copy(
-                    out=grp[i][:, 0:nv, :].rearrange("p (c i) t -> p c t i", i=4),
-                    in_=w1raw[i][:, :, 0:nv].rearrange("p t (c i) -> p c t i", i=4),
-                )
-                if i not in PE_TILES:
-                    nc.scalar.copy(
-                        out=grp[i][:, nv:HID, :].rearrange("p (c i) t -> p c t i", i=4),
-                        in_=w1raw[i][:, :, nv:HID].rearrange("p t (c i) -> p c t i", i=4),
-                    )
+                parts = PARTS.get(i, 1)
+                w = HID // parts
+                for h in range(parts) if only is None else [only]:
+                    end = w - (tail if h == parts - 1 else 0)
+                    nv = end - S_COLS_A[i] // parts
+                    for copy, a, b in ((nc.vector.tensor_copy, 0, nv), (nc.scalar.copy, nv, end)):
+                        if a < b:
+                            copy(
+                                out=grp[i][:, h * w + a : h * w + b, :].rearrange("p (c i) t -> p c t i", i=4),
+                                in_=w1raw[i][:, h, :, a:b].rearrange("p t (c i) -> p c t i", i=4),
+                            )
             else:
                 u = i - G
                 dt, q = unit(u)
-                rv = 8 - S_ROWS_B[u]
+                end = 8 - tail // P
+                rv = end - S_ROWS_B[u]
                 dsl = slice(dt * P, (dt + 1) * P)
                 nc.vector.tensor_copy(
                     out=grp[i][:, 0 : rv * P, :].rearrange("p (r c i) t -> p r c t i", r=rv, i=4),
                     in_=w2raw[:, 8 * q : 8 * q + rv, :, dsl].rearrange("p r t (c i) -> p r c t i", i=4),
                 )
-                for r in range(rv, 6 if i in PE_TILES else 8):
+                for r in range(rv, end):
                     nc.scalar.copy(
                         out=grp[i][:, r * P : (r + 1) * P, :].rearrange("p (c i) t -> p c t i", i=4),
                         in_=w2raw[:, 8 * q + r, :, dsl].rearrange("p t (c i) -> p c t i", i=4),
                     )
 
+        def regroup_pe_evac(i):
             if i in PE_TILES:
                 nc.scalar.copy(out=grp[i][:, HID - PE_W : HID, :], in_=pg[i][:])
 
@@ -138,15 +155,15 @@ def tile_blockresmlp_mixerblock_pa_kernel(tc, y_lanes, w1, b1, w2, b2, out):
 
         def z_transposes(m):
             gp, bt = m // 2, m % 2
-            zt[m] = psum.tile([P, 4, P], F32, name="zt%d" % m, tag="zt")
+            zt[m] = psum.tile([P, 4, P], F32, name="zt%d" % m, tag="tr")
             yw = y_sb[bt][:].bitcast(F32).rearrange("b (p j w) -> b j w p", j=4, w=4)
             for j in range(4):
                 nc.tensor.transpose(out=zt[m][:, j, :], in_=yw[:, j, gp, :], identity=ident_f[:])
 
         def z_evac(m):
             gp, bt = m // 2, m % 2
-            if bt == 0:
-                zg[gp] = work.tile([P, 2, BS, 4], BF16, name="zg%d" % gp, tag="zg", align_bytes=64)
+            if gp not in zg:
+                zg[gp] = zh_pool.tile([P, 2, BS, 4], BF16, name="zg%d" % gp, tag="zh", align_bytes=64)
             src = zt[m][:].rearrange("p j b -> p (j b)").bitcast(BF16).rearrange(
                 "p (j b e) -> p e b j", j=4, e=2
             )
@@ -160,7 +177,7 @@ def tile_blockresmlp_mixerblock_pa_kernel(tc, y_lanes, w1, b1, w2, b2, out):
             )
 
         def mm1(g, k):
-            hp[(g, k)] = psum.tile([P, 2, BS], F32, name="hp%d_%d" % (g, k), tag="acc", bufs=4)
+            hp[(g, k)] = psum.tile([P, 2, BS], F32, name="hp%d_%d" % (g, k), tag="acc")
             for h in range(2):
                 t = 2 * k + h
                 nc.tensor.matmul_mx(
@@ -191,7 +208,7 @@ def tile_blockresmlp_mixerblock_pa_kernel(tc, y_lanes, w1, b1, w2, b2, out):
 
         def elu_combine(g, c):
             if c == 0:
-                hg[g] = work.tile([P, 2, BS, 4], BF16, name="hg%d" % g, tag="hg", align_bytes=64)
+                hg[g] = zh_pool.tile([P, 2, BS, 4], BF16, name="hg%d" % g, tag="zh", align_bytes=64)
             nc.vector.scalar_tensor_tensor(
                 out=hg[g][:, c, :, :],
                 in0=e_t[(g, c)][:].rearrange("p j b -> p b j"),
@@ -212,7 +229,7 @@ def tile_blockresmlp_mixerblock_pa_kernel(tc, y_lanes, w1, b1, w2, b2, out):
             dt, q = unit(u)
             i = u + G
             for half in range(2):
-                rp[(u, half)] = psum.tile([P, 2, BS], F32, name="rp%d_%d" % (u, half), tag="acc", bufs=4)
+                rp[(u, half)] = psum.tile([P, 2, BS], F32, name="rp%d_%d" % (u, half), tag="acc")
                 for h in range(2):
                     gl = 2 * half + h
                     g = 4 * q + gl
@@ -233,17 +250,19 @@ def tile_blockresmlp_mixerblock_pa_kernel(tc, y_lanes, w1, b1, w2, b2, out):
             t_t[u] = work.tile([P, 4, BS], F32, name="t%d" % u, tag="t")
             for gl in range(4):
                 col = 64 + 4 * (4 * q + gl) + dt
-                nc.scalar.activation(
-                    out=t_t[u][:, gl, :],
-                    in_=rp[(u, gl // 2)][:, gl % 2, :],
-                    func=ACT.Identity,
-                    bias=bT[:, col : col + 1],
-                    scale=1.0,
-                )
+                src = rp[(u, gl // 2)][:, gl % 2, :]
+                if u == 7 and gl >= 2:
+                    nc.vector.tensor_scalar(
+                        out=t_t[u][:, gl, :], in0=src, scalar1=bT[:, col : col + 1], scalar2=None, op0=ALU.add
+                    )
+                else:
+                    nc.scalar.activation(
+                        out=t_t[u][:, gl, :], in_=src, func=ACT.Identity, bias=bT[:, col : col + 1], scale=1.0
+                    )
 
         def out_transposes(u):
             for bt in range(2):
-                ot[(u, bt)] = psum.tile([P, 4, P], F32, name="ot%d_%d" % (u, bt), tag="ot")
+                ot[(u, bt)] = psum.tile([P, 4, P], F32, name="ot%d_%d" % (u, bt), tag="tr")
                 for gl in range(4):
                     nc.tensor.transpose(
                         out=ot[(u, bt)][:, gl, :],
@@ -269,75 +288,84 @@ def tile_blockresmlp_mixerblock_pa_kernel(tc, y_lanes, w1, b1, w2, b2, out):
                         in_=osb[dt][:, bt, :, :].rearrange("p d g -> p (d g)"),
                     )
 
+        nc.vector.memset(warm[:], 0.0)
+        nc.scalar.activation(out=warm[:], in_=warm[:], func=ACT.Exp, scale=1.0)
         load_w1(0)
-        for bt in range(2):
-            nc.sync.dma_start(out=y_sb[bt][:], in_=y_lanes[bt * P : (bt + 1) * P, :])
+        nc.sync.dma_start(out=y_sb[0][:], in_=y_lanes[0:P, :])
+        load_w1(1)
         nc.vector.memset(brow[96:128, :], 0.0)
         nc.sync.dma_start(out=brow[0:64, :], in_=b1.rearrange("g o (t p) -> (g o t) p", p=P))
         nc.sync.dma_start(out=brow[64:96, :], in_=b2.rearrange("g o (t p) -> (g o t) p", p=P))
-        load_w1(1)
+        nc.sync.dma_start(out=y_sb[1][:], in_=y_lanes[P : 2 * P, :])
         load_w1(2)
 
-        regroup(0)
-        load_w1(3)
-        quant_w(0)
-        z_transposes(0)
-        z_evac(0)
-        z_transposes(1)
-        z_evac(1)
-        bps = psum.tile([P, P], BF16, name="bps", tag="zt")
+        for i in range(AHEAD):
+            regroup(i)
+            quant_w(i)
+            load_w1(i + 3)
+        for m in (0, 2, 4, 6):
+            z_transposes(m)
+            z_evac(m)
+        bps = psum.tile([P, P], BF16, name="bps", tag="tr")
         nc.tensor.transpose(out=bps[:], in_=brow[:], identity=ident_b[:])
-        nc.vector.tensor_copy(out=bT[:], in_=bps[:, 0:96])
-        z_transposes(2)
-        z_evac(2)
+        nc.scalar.copy(out=bT[:], in_=bps[:, 0:96])
+        for m in (1, 3):
+            z_transposes(m)
+            z_evac(m)
+        regroup(AHEAD, 0)
         quant_z(0)
+        regroup_pe(AHEAD)
         for k in range(4):
             mm1(0, k)
-        regroup(1)
-        load_w1(4)
+        regroup(AHEAD, 1)
+        regroup_pe_evac(AHEAD)
+        quant_z(1)
+        load_w1(AHEAD + 3)
         load_w2(0)
         load_w2(1)
 
         for s in range(N_UNITS + 1):
             u = s - G
-            if s + 1 < N_UNITS:
-                quant_w(s + 1)
+            i = s + AHEAD + 1
+            if i - 1 < N_UNITS:
+                quant_w(i - 1)
+            if s in (1, 2):
+                quant_z(s + 1)
             if 1 <= s <= G:
                 elu_combine(s - 1, 1)
-            if s + 2 < N_UNITS:
-                regroup_pe(s + 2)
+            if s >= G and u < G:
+                mm2(u)
+            if i < N_UNITS:
+                regroup_pe(i)
             if s < G:
-                if s <= 4:
-                    z_transposes(s + 3)
+                if s < 2:
+                    z_transposes(2 * s + 5)
                 for k in range(2):
                     elu_scalar(s, k)
                     if s + 1 < G:
                         mm1(s + 1, k)
-            else:
-                if u < G:
-                    mm2(u)
-                if u >= 1:
-                    out_transposes(u - 1)
-            if s + 2 < N_UNITS:
-                regroup(s + 2)
-                if s + 5 < G:
-                    load_w1(s + 5)
+            elif u >= 1:
+                out_transposes(u - 1)
+            if i < N_UNITS:
+                regroup(i)
+                if i + 3 < G:
+                    load_w1(i + 3)
+                if 2 * s + 3 < G:
                     load_w2(2 * s + 2)
                     load_w2(2 * s + 3)
-            if s <= 4:
-                z_evac(s + 3)
+            if s < 2:
+                z_evac(2 * s + 5)
+            if s >= G and u < G:
+                out_evac(u)
+            if i < N_UNITS:
+                regroup_pe_evac(i)
             if 1 <= s <= G:
                 quant_h(s - 1)
-            if s in (0, 2, 4):
-                quant_z(s // 2 + 1)
             if s < G:
                 for k in range(2, 4):
                     elu_scalar(s, k)
                     if s + 1 < G:
                         mm1(s + 1, k)
                 elu_combine(s, 0)
-            else:
-                if u < G:
-                    out_evac(u)
-                if u >= 1:
-                    out_add(u - 1)
+            elif u >= 1:
+                out_add(u - 1)

@@ -18,7 +18,8 @@ FLOPS = 2 * G * BS * BLOCK * HID * 2
 N_UNITS = 16
 S_COLS_A = [0,0,0,64,64,64,64,64]
 S_ROWS_B = [2,2,2,2,4,2,4,4]
-PE_TILES = range(2, 14)
+V_RUN, S_RUN = 8, 4
+PE_TILES = {2: 1, 3: 1, 4: 1, 5: 1, 6: 1, 7: 1, 8: 1, 9: 1, 10: 1, 11: 1, 12: 1, 13: 1}
 PE_W = 256
 AHEAD = 2
 PARTS = {0: 2, 2: 2}
@@ -89,19 +90,19 @@ def tile_blockresmlp_mixerblock_pa_kernel(tc, y_lanes, w1, b1, w2, b2, out):
             )
 
         def regroup_pe(i):
-            if i not in PE_TILES:
-                return
-            pg[i] = psum.tile([P, PE_W, 4], BF16, name="pg%d" % i, tag="tr")
-            for h in range(PE_W // P):
+            for h in range(2 * PE_TILES.get(i, 0)):
+                if h % 2 == 0:
+                    pg[(i, h // 2)] = psum.tile([P, PE_W, 4], BF16, name="pg%d_%d" % (i, h), tag="tr")
+                back = (2 * PE_TILES[i] - h) * P
                 if i < G:
-                    w = HID // PARTS.get(i, 1)
-                    lo = w - PE_W + h * P
+                    lo = HID // PARTS.get(i, 1) - back
                     src = w1raw[i][:, PARTS.get(i, 1) - 1, :, lo : lo + P]
                 else:
                     dt, q = unit(i - G)
-                    src = w2raw[:, 8 * q + 8 - PE_W // P + h, :, dt * P : (dt + 1) * P]
+                    src = w2raw[:, 8 * q + 8 - back // P, :, dt * P : (dt + 1) * P]
+                lo = h % 2 * P
                 nc.tensor.matmul(
-                    out=pg[i][:, h * P : (h + 1) * P, :].rearrange("p (c i) t -> p c t i", i=4),
+                    out=pg[(i, h // 2)][:, lo : lo + P, :].rearrange("p (c i) t -> p c t i", i=4),
                     lhsT=ident_b[:],
                     rhs=src.rearrange("p t (c i) -> p c t i", i=4),
                     start=True,
@@ -111,18 +112,18 @@ def tile_blockresmlp_mixerblock_pa_kernel(tc, y_lanes, w1, b1, w2, b2, out):
         def regroup(i, only=None):
             if i not in grp:
                 grp[i] = grp_pool.tile([P, 1024, 4], BF16, name="grp%d" % i, tag="grp", align_bytes=64)
-            tail = PE_W if i in PE_TILES else 0
+            tail = PE_W * PE_TILES.get(i, 0)
             if i < G:
                 parts = PARTS.get(i, 1)
                 w = HID // parts
                 for h in range(parts) if only is None else [only]:
                     end = w - (tail if h == parts - 1 else 0)
                     nv = end - S_COLS_A[i] // parts
-                    for copy, a, b in ((nc.vector.tensor_copy, 0, nv), (nc.scalar.copy, nv, end)):
+                    for copy, a, b, run in ((nc.vector.tensor_copy, 0, nv, V_RUN), (nc.scalar.copy, nv, end, S_RUN)):
                         if a < b:
                             copy(
-                                out=grp[i][:, h * w + a : h * w + b, :].rearrange("p (c i) t -> p c t i", i=4),
-                                in_=w1raw[i][:, h, :, a:b].rearrange("p t (c i) -> p c t i", i=4),
+                                out=grp[i][:, h * w + a : h * w + b, :].rearrange("p (c i) t -> p c t i", i=run),
+                                in_=w1raw[i][:, h, :, a:b].rearrange("p t (c i) -> p c t i", i=run),
                             )
             else:
                 u = i - G
@@ -131,8 +132,8 @@ def tile_blockresmlp_mixerblock_pa_kernel(tc, y_lanes, w1, b1, w2, b2, out):
                 rv = end - S_ROWS_B[u]
                 dsl = slice(dt * P, (dt + 1) * P)
                 nc.vector.tensor_copy(
-                    out=grp[i][:, 0 : rv * P, :].rearrange("p (r c i) t -> p r c t i", r=rv, i=4),
-                    in_=w2raw[:, 8 * q : 8 * q + rv, :, dsl].rearrange("p r t (c i) -> p r c t i", i=4),
+                    out=grp[i][:, 0 : rv * P, :].rearrange("p (r c i) t -> p r c t i", r=rv, i=V_RUN),
+                    in_=w2raw[:, 8 * q : 8 * q + rv, :, dsl].rearrange("p r t (c i) -> p r c t i", i=V_RUN),
                 )
                 for r in range(rv, end):
                     nc.scalar.copy(
@@ -141,8 +142,10 @@ def tile_blockresmlp_mixerblock_pa_kernel(tc, y_lanes, w1, b1, w2, b2, out):
                     )
 
         def regroup_pe_evac(i):
-            if i in PE_TILES:
-                nc.scalar.copy(out=grp[i][:, HID - PE_W : HID, :], in_=pg[i][:])
+            n = PE_TILES.get(i, 0)
+            for h in range(n):
+                lo = HID - (n - h) * PE_W
+                nc.scalar.copy(out=grp[i][:, lo : lo + PE_W, :], in_=pg[(i, h)][:])
 
         def quant_w(i):
             wc[i] = code_pool.tile([P, 1024], U32, name="wc%d" % i, tag="wc", align_bytes=64)
@@ -250,15 +253,13 @@ def tile_blockresmlp_mixerblock_pa_kernel(tc, y_lanes, w1, b1, w2, b2, out):
             t_t[u] = work.tile([P, 4, BS], F32, name="t%d" % u, tag="t")
             for gl in range(4):
                 col = 64 + 4 * (4 * q + gl) + dt
-                src = rp[(u, gl // 2)][:, gl % 2, :]
-                if u == 7 and gl >= 2:
-                    nc.vector.tensor_scalar(
-                        out=t_t[u][:, gl, :], in0=src, scalar1=bT[:, col : col + 1], scalar2=None, op0=ALU.add
-                    )
-                else:
-                    nc.scalar.activation(
-                        out=t_t[u][:, gl, :], in_=src, func=ACT.Identity, bias=bT[:, col : col + 1], scale=1.0
-                    )
+                nc.scalar.activation(
+                    out=t_t[u][:, gl, :],
+                    in_=rp[(u, gl // 2)][:, gl % 2, :],
+                    func=ACT.Identity,
+                    bias=bT[:, col : col + 1],
+                    scale=1.0,
+                )
 
         def out_transposes(u):
             for bt in range(2):

from contextlib import ExitStack

import concourse.mybir as mybir
from concourse.masks import make_identity

F32 = mybir.dt.float32
BF16 = mybir.dt.bfloat16
U32 = mybir.dt.uint32
U8 = mybir.dt.uint8
FP8X4 = mybir.dt.float8_e4m3fn_x4
ACT = mybir.ActivationFunctionType
ALU = mybir.AluOpType

P = 128
BS, BLOCK, HID, G = 256, 512, 1024, 8
FLOPS = 2 * G * BS * BLOCK * HID * 2

N_UNITS = 16
S_COLS_A = [0,0,0,64,64,64,64,64]
S_ROWS_B = [2,2,2,2,4,2,4,4]
V_RUN, S_RUN = 8, 4
PE_TILES = {2: 1, 3: 1, 4: 1, 5: 1, 6: 1, 7: 1, 8: 1, 9: 1, 10: 1, 11: 1, 12: 1, 13: 1}
PE_W = 256
AHEAD = 2
PARTS = {0: 2, 2: 2}
UNITS = [(0, 0), (1, 0), (0, 1), (1, 1), (2, 0), (2, 1), (3, 0), (3, 1)]


def tile_blockresmlp_mixerblock_pa_kernel(tc, y_lanes, w1, b1, w2, b2, out):
    nc = tc.nc
    with ExitStack() as ctx:
        const = ctx.enter_context(tc.tile_pool(name="const", bufs=1))
        raw_pool = ctx.enter_context(tc.tile_pool(name="raw", bufs=3))
        grp_pool = ctx.enter_context(tc.tile_pool(name="grp", bufs=3))
        code_pool = ctx.enter_context(tc.tile_pool(name="code", bufs=3))
        act_pool = ctx.enter_context(tc.tile_pool(name="act", bufs=3))
        zh_pool = ctx.enter_context(tc.tile_pool(name="zh", bufs=4))
        work = ctx.enter_context(tc.tile_pool(name="work", bufs=2))
        psum = ctx.enter_context(tc.psum_pool(name="psum", bufs=4))
        ctx.enter_context(tc.manual_schedule())

        ident_b = const.tile([P, P], BF16, name="ident_b")
        ident_f = const.tile([P, P], F32, name="ident_f")
        make_identity(nc, ident_f[:])
        make_identity(nc, ident_b[:])

        y_sb = [const.tile([P, BLOCK * G], BF16, name="y_sb%d" % bt) for bt in range(2)]
        w2raw = const.tile([P, 2 * G, 4, BLOCK], BF16, name="w2raw")
        zc = const.tile([P, G, BS], U32, name="zc", align_bytes=64)
        zs = const.tile([P, G, BS], U8, name="zs", align_bytes=64)
        hc = const.tile([P, G, 2 * BS], U32, name="hc", align_bytes=64)
        hs = const.tile([P, G, 2 * BS], U8, name="hs", align_bytes=64)
        brow = const.tile([P, P], BF16, name="brow")
        bT = const.tile([P, 96], F32, name="bT")
        warm = const.tile([P, 1], F32, name="warm")

        w1raw = {}
        grp = {}
        wc = {}
        ws = {}
        pg = {}
        zt = {}
        zg = {}
        hp = {}
        e_t = {}
        r_t = {}
        hg = {}
        rp = {}
        t_t = {}
        ot = {}
        osb = {}

        def unit(u):
            return UNITS[u]

        def load_w1(g):
            parts = PARTS.get(g, 1)
            w = HID // parts
            w1raw[g] = raw_pool.tile([P, parts, 4, w], BF16, name="w1raw%d" % g, tag="w1raw")
            for h in range(parts):
                nc.sync.dma_start(
                    out=w1raw[g][:, h, :, :],
                    in_=w1[g].rearrange("(p j) n -> p j n", j=4)[:, :, h * w : (h + 1) * w],
                )

        def load_w2(g):
            nc.sync.dma_start(
                out=w2raw[:, 2 * g : 2 * g + 2, :, :],
                in_=w2[g].rearrange("(c j p) d -> p c j d", c=2, j=4),
            )

        def regroup_pe(i):
            for h in range(2 * PE_TILES.get(i, 0)):
                if h % 2 == 0:
                    pg[(i, h // 2)] = psum.tile([P, PE_W, 4], BF16, name="pg%d_%d" % (i, h), tag="tr")
                back = (2 * PE_TILES[i] - h) * P
                if i < G:
                    lo = HID // PARTS.get(i, 1) - back
                    src = w1raw[i][:, PARTS.get(i, 1) - 1, :, lo : lo + P]
                else:
                    dt, q = unit(i - G)
                    src = w2raw[:, 8 * q + 8 - back // P, :, dt * P : (dt + 1) * P]
                lo = h % 2 * P
                nc.tensor.matmul(
                    out=pg[(i, h // 2)][:, lo : lo + P, :].rearrange("p (c i) t -> p c t i", i=4),
                    lhsT=ident_b[:],
                    rhs=src.rearrange("p t (c i) -> p c t i", i=4),
                    start=True,
                    stop=True,
                )

        def regroup(i, only=None):
            if i not in grp:
                grp[i] = grp_pool.tile([P, 1024, 4], BF16, name="grp%d" % i, tag="grp", align_bytes=64)
            tail = PE_W * PE_TILES.get(i, 0)
            if i < G:
                parts = PARTS.get(i, 1)
                w = HID // parts
                for h in range(parts) if only is None else [only]:
                    end = w - (tail if h == parts - 1 else 0)
                    nv = end - S_COLS_A[i] // parts
                    for copy, a, b, run in ((nc.vector.tensor_copy, 0, nv, V_RUN), (nc.scalar.copy, nv, end, S_RUN)):
                        if a < b:
                            copy(
                                out=grp[i][:, h * w + a : h * w + b, :].rearrange("p (c i) t -> p c t i", i=run),
                                in_=w1raw[i][:, h, :, a:b].rearrange("p t (c i) -> p c t i", i=run),
                            )
            else:
                u = i - G
                dt, q = unit(u)
                end = 8 - tail // P
                rv = end - S_ROWS_B[u]
                dsl = slice(dt * P, (dt + 1) * P)
                nc.vector.tensor_copy(
                    out=grp[i][:, 0 : rv * P, :].rearrange("p (r c i) t -> p r c t i", r=rv, i=V_RUN),
                    in_=w2raw[:, 8 * q : 8 * q + rv, :, dsl].rearrange("p r t (c i) -> p r c t i", i=V_RUN),
                )
                for r in range(rv, end):
                    nc.scalar.copy(
                        out=grp[i][:, r * P : (r + 1) * P, :].rearrange("p (c i) t -> p c t i", i=4),
                        in_=w2raw[:, 8 * q + r, :, dsl].rearrange("p t (c i) -> p c t i", i=4),
                    )

        def regroup_pe_evac(i):
            n = PE_TILES.get(i, 0)
            for h in range(n):
                lo = HID - (n - h) * PE_W
                nc.scalar.copy(out=grp[i][:, lo : lo + PE_W, :], in_=pg[(i, h)][:])

        def quant_w(i):
            wc[i] = code_pool.tile([P, 1024], U32, name="wc%d" % i, tag="wc", align_bytes=64)
            ws[i] = code_pool.tile([P, 1024], U8, name="ws%d" % i, tag="ws", align_bytes=64)
            nc.vector.quantize_mx(
                out=wc[i][:].bitcast(FP8X4),
                scales=ws[i][:],
                in_=grp[i][:].rearrange("p n j -> p (n j)"),
            )

        def z_transposes(m):
            gp, bt = m // 2, m % 2
            zt[m] = psum.tile([P, 4, P], F32, name="zt%d" % m, tag="tr")
            yw = y_sb[bt][:].bitcast(F32).rearrange("b (p j w) -> b j w p", j=4, w=4)
            for j in range(4):
                nc.tensor.transpose(out=zt[m][:, j, :], in_=yw[:, j, gp, :], identity=ident_f[:])

        def z_evac(m):
            gp, bt = m // 2, m % 2
            if gp not in zg:
                zg[gp] = zh_pool.tile([P, 2, BS, 4], BF16, name="zg%d" % gp, tag="zh", align_bytes=64)
            src = zt[m][:].rearrange("p j b -> p (j b)").bitcast(BF16).rearrange(
                "p (j b e) -> p e b j", j=4, e=2
            )
            nc.scalar.copy(out=zg[gp][:, :, bt * P : (bt + 1) * P, :], in_=src)

        def quant_z(gp):
            nc.vector.quantize_mx(
                out=zc[:, 2 * gp : 2 * gp + 2, :].rearrange("p g b -> p (g b)").bitcast(FP8X4),
                scales=zs[:, 2 * gp : 2 * gp + 2, :].rearrange("p g b -> p (g b)"),
                in_=zg[gp][:].rearrange("p e b j -> p (e b j)"),
            )

        def mm1(g, k):
            hp[(g, k)] = psum.tile([P, 2, BS], F32, name="hp%d_%d" % (g, k), tag="acc")
            for h in range(2):
                t = 2 * k + h
                nc.tensor.matmul_mx(
                    out=hp[(g, k)][:, h, :],
                    lhsT=wc[g][:, t * P : (t + 1) * P].bitcast(FP8X4),
                    lhsT_scale=ws[g][:, t * P : (t + 1) * P],
                    rhs=zc[:, g, :].bitcast(FP8X4),
                    rhs_scale=zs[:, g, :],
                    start=True,
                    stop=True,
                )

        def elu_scalar(g, k):
            c = k // 2
            if k % 2 == 0:
                e_t[(g, c)] = act_pool.tile([P, 4, BS], F32, name="e%d_%d" % (g, c), tag="e")
                r_t[(g, c)] = act_pool.tile([P, 4, BS], BF16, name="r%d_%d" % (g, c), tag="r")
            for h in range(2):
                t = 2 * k + h
                j = t % 4
                bias = bT[:, 8 * g + t : 8 * g + t + 1]
                nc.scalar.activation(
                    out=e_t[(g, c)][:, j, :], in_=hp[(g, k)][:, h, :], func=ACT.Exp, bias=bias, scale=1.0
                )
                nc.scalar.activation(
                    out=r_t[(g, c)][:, j, :], in_=hp[(g, k)][:, h, :], func=ACT.Relu, bias=bias, scale=1.0
                )

        def elu_combine(g, c):
            if c == 0:
                hg[g] = zh_pool.tile([P, 2, BS, 4], BF16, name="hg%d" % g, tag="zh", align_bytes=64)
            nc.vector.scalar_tensor_tensor(
                out=hg[g][:, c, :, :],
                in0=e_t[(g, c)][:].rearrange("p j b -> p b j"),
                scalar=-1.0,
                in1=r_t[(g, c)][:].rearrange("p j b -> p b j"),
                op0=ALU.add,
                op1=ALU.min,
            )

        def quant_h(g):
            nc.vector.quantize_mx(
                out=hc[:, g, :].bitcast(FP8X4),
                scales=hs[:, g, :],
                in_=hg[g][:].rearrange("p c b j -> p (c b j)"),
            )

        def mm2(u):
            dt, q = unit(u)
            i = u + G
            for half in range(2):
                rp[(u, half)] = psum.tile([P, 2, BS], F32, name="rp%d_%d" % (u, half), tag="acc")
                for h in range(2):
                    gl = 2 * half + h
                    g = 4 * q + gl
                    for c in range(2):
                        r = 2 * gl + c
                        nc.tensor.matmul_mx(
                            out=rp[(u, half)][:, h, :],
                            lhsT=wc[i][:, r * P : (r + 1) * P].bitcast(FP8X4),
                            lhsT_scale=ws[i][:, r * P : (r + 1) * P],
                            rhs=hc[:, g, c * BS : (c + 1) * BS].bitcast(FP8X4),
                            rhs_scale=hs[:, g, c * BS : (c + 1) * BS],
                            start=(c == 0),
                            stop=(c == 1),
                        )

        def out_evac(u):
            dt, q = unit(u)
            t_t[u] = work.tile([P, 4, BS], F32, name="t%d" % u, tag="t")
            for gl in range(4):
                col = 64 + 4 * (4 * q + gl) + dt
                nc.scalar.activation(
                    out=t_t[u][:, gl, :],
                    in_=rp[(u, gl // 2)][:, gl % 2, :],
                    func=ACT.Identity,
                    bias=bT[:, col : col + 1],
                    scale=1.0,
                )

        def out_transposes(u):
            for bt in range(2):
                ot[(u, bt)] = psum.tile([P, 4, P], F32, name="ot%d_%d" % (u, bt), tag="tr")
                for gl in range(4):
                    nc.tensor.transpose(
                        out=ot[(u, bt)][:, gl, :],
                        in_=t_t[u][:, gl, bt * P : (bt + 1) * P],
                        identity=ident_f[:],
                    )

        def out_add(u):
            dt, q = unit(u)
            if q == 0:
                osb[dt] = work.tile([P, 2, P, G], F32, name="osb%d" % dt, tag="osb")
            for bt in range(2):
                yv = y_sb[bt][:].rearrange("b (d g) -> b d g", g=G)
                nc.vector.tensor_tensor(
                    out=osb[dt][:, bt, :, 4 * q : 4 * q + 4],
                    in0=ot[(u, bt)][:].rearrange("p g d -> p d g"),
                    in1=yv[:, dt * P : (dt + 1) * P, 4 * q : 4 * q + 4],
                    op=ALU.add,
                )
                if q == 1:
                    nc.sync.dma_start(
                        out=out[bt * P : (bt + 1) * P, dt * P * G : (dt + 1) * P * G],
                        in_=osb[dt][:, bt, :, :].rearrange("p d g -> p (d g)"),
                    )

        nc.vector.memset(warm[:], 0.0)
        nc.scalar.activation(out=warm[:], in_=warm[:], func=ACT.Exp, scale=1.0)
        load_w1(0)
        nc.sync.dma_start(out=y_sb[0][:], in_=y_lanes[0:P, :])
        load_w1(1)
        nc.vector.memset(brow[96:128, :], 0.0)
        nc.sync.dma_start(out=brow[0:64, :], in_=b1.rearrange("g o (t p) -> (g o t) p", p=P))
        nc.sync.dma_start(out=brow[64:96, :], in_=b2.rearrange("g o (t p) -> (g o t) p", p=P))
        nc.sync.dma_start(out=y_sb[1][:], in_=y_lanes[P : 2 * P, :])
        load_w1(2)

        for i in range(AHEAD):
            regroup(i)
            quant_w(i)
            load_w1(i + 3)
        for m in (0, 2, 4, 6):
            z_transposes(m)
            z_evac(m)
        bps = psum.tile([P, P], BF16, name="bps", tag="tr")
        nc.tensor.transpose(out=bps[:], in_=brow[:], identity=ident_b[:])
        nc.scalar.copy(out=bT[:], in_=bps[:, 0:96])
        for m in (1, 3):
            z_transposes(m)
            z_evac(m)
        regroup(AHEAD, 0)
        quant_z(0)
        regroup_pe(AHEAD)
        for k in range(4):
            mm1(0, k)
        regroup(AHEAD, 1)
        regroup_pe_evac(AHEAD)
        quant_z(1)
        load_w1(AHEAD + 3)
        load_w2(0)
        load_w2(1)

        for s in range(N_UNITS + 1):
            u = s - G
            i = s + AHEAD + 1
            if i - 1 < N_UNITS:
                quant_w(i - 1)
            if s in (1, 2):
                quant_z(s + 1)
            if 1 <= s <= G:
                elu_combine(s - 1, 1)
            if s >= G and u < G:
                mm2(u)
            if i < N_UNITS:
                regroup_pe(i)
            if s < G:
                if s < 2:
                    z_transposes(2 * s + 5)
                for k in range(2):
                    elu_scalar(s, k)
                    if s + 1 < G:
                        mm1(s + 1, k)
            elif u >= 1:
                out_transposes(u - 1)
            if i < N_UNITS:
                regroup(i)
                if i + 3 < G:
                    load_w1(i + 3)
                if 2 * s + 3 < G:
                    load_w2(2 * s + 2)
                    load_w2(2 * s + 3)
            if s < 2:
                z_evac(2 * s + 5)
            if s >= G and u < G:
                out_evac(u)
            if i < N_UNITS:
                regroup_pe_evac(i)
            if 1 <= s <= G:
                quant_h(s - 1)
            if s < G:
                for k in range(2, 4):
                    elu_scalar(s, k)
                    if s + 1 < G:
                        mm1(s + 1, k)
                elu_combine(s, 0)
            elif u >= 1:
                out_add(u - 1)
